import numpy as np
import ml_dtypes


def mxq(x, axis, fmt="e4m3"):
    dtype, down = {"e4m3": (ml_dtypes.float8_e4m3fn, 7), "e5m2": (ml_dtypes.float8_e5m2, 14)}[fmt]
    v = np.moveaxis(np.asarray(x, np.float32).astype(ml_dtypes.bfloat16).astype(np.float64), axis, -1)
    blocks = v.reshape(v.shape[:-1] + (-1, 32))
    amax = np.abs(blocks).max(-1, keepdims=True)
    byte = np.maximum(np.where(amax > 0, np.frexp(amax)[1] - 1 + 127, 0) - down, 1)
    scale = np.exp2(byte - 127.0)
    codes = (blocks / scale).astype(np.float32).astype(dtype).astype(np.float64)
    return np.moveaxis((codes * scale).reshape(v.shape), -1, axis)


WIDE = False


def mx_kscale(k):
    if not WIDE:
        return np.ones(k)
    levels = np.array([10, -10, 5, -5, 0])
    if k % 512:
        return np.exp2(np.random.permutation(np.resize(levels, k // 32))).repeat(32)
    a = np.empty((k // 512, 16))
    for p in range(k // 512):
        a[p, :8] = np.random.permutation(np.resize(levels, 8))
        for g in range(8):
            far = levels[np.abs(levels - a[p, g]) >= 10]
            a[p, g + 8] = far[np.random.randint(len(far))]
    return np.exp2(a.ravel()).repeat(32)


BF16 = ml_dtypes.bfloat16


def bf(x):
    return np.asarray(x, np.float32).astype(BF16)


def f64(x):
    return np.asarray(x).astype(np.float64)


B, C, D, T, H, W, P = 1, 1024, 512, 8, 16, 16, 2
N = T * H * W
NP = T * (H // P) * (W // P)


def conv1x1(wq, b, xq):
    return ((wq @ xq) + b[None, :, None]).reshape(B, D, T, H, W)


def maxpool(v):
    return v.reshape(B, D, T, H // P, P, W // P, P).max(axis=(4, 6))


def draw0():
    s = mx_kscale(C)
    a = 1.0 / np.sqrt(C) / s[None, :]
    return {"x": bf(np.random.standard_normal((B, C, T, H, W)) * s[None, :, None, None, None]),
            "g_w": bf(np.random.standard_normal((D, C)) * 0.15 * a),
            "g_b": bf(np.random.standard_normal(D) * 0.03),
            "theta_w": bf(np.random.standard_normal((D, C)) * 2.0 * a),
            "theta_b": bf(np.random.standard_normal(D) * 0.2),
            "phi_w": bf(np.random.standard_normal((D, C)) * a),
            "phi_b": bf(np.random.standard_normal(D) * 0.1)}


def core(x, g_w, g_b, theta_w, theta_b, phi_w, phi_b):
    xq = mxq(f64(x).reshape(B, C, N), 1, "e4m3")
    g_x = maxpool(conv1x1(mxq(f64(g_w), 1, "e4m3"), f64(g_b), xq)).reshape(B, D, NP)
    theta_x = conv1x1(mxq(f64(theta_w), 1, "e4m3"), f64(theta_b), xq).reshape(B, D, N)
    phi_x = maxpool(conv1x1(mxq(f64(phi_w), 1, "e4m3"), f64(phi_b), xq)).reshape(B, D, NP)
    return g_x, theta_x, phi_x


def e4m3fn_bytes(y):
    return np.clip(np.asarray(y, np.float64), -448.0, 448.0).astype(np.float32).astype(ml_dtypes.float8_e4m3fn).view(np.uint8)


def e4m3fn_values(b):
    return np.asarray(b, np.uint8).view(ml_dtypes.float8_e4m3fn).astype(np.float64)


def setup_inputs():
    d = draw0()
    x0 = np.asarray(d['x']).astype(np.float64)
    s = (np.max(np.abs(x0), axis=(0, 2, 3, 4), keepdims=True) / 448.0).astype(np.float32)
    out = {}
    for k, v in d.items():
        if k == 'x':
            out['x_bytes'] = e4m3fn_bytes(x0 / s.astype(np.float64))
            out['x_scale'] = s
        else:
            out[k] = v
    return out


def reference(x_bytes, x_scale, g_w, g_b, theta_w, theta_b, phi_w, phi_b):
    return core(e4m3fn_values(x_bytes) * x_scale.astype(np.float64), g_w, g_b, theta_w, theta_b, phi_w, phi_b)

@@ -1,0 +1,288 @@
+from contextlib import ExitStack
+
+import concourse.mybir as mybir
+from concourse.masks import make_identity
+
+F32 = mybir.dt.float32
+BF16 = mybir.dt.bfloat16
+U32 = mybir.dt.uint32
+U8 = mybir.dt.uint8
+FP8 = mybir.dt.float8_e4m3fn
+FP8X4 = mybir.dt.float8_e4m3fn_x4
+ACT = mybir.ActivationFunctionType
+ALU = mybir.AluOpType
+AX = mybir.AxisListType
+
+P = 128
+PACK = 4
+PASSES = 2
+CHUNK = 512
+CHUNKS = 4
+POOLED = CHUNK // 4
+M_TILES = 4
+TILES = 3 * M_TILES
+THETA, G, PHI = 0, 1, 2
+RUN = 4
+HALVES = 2
+
+FLOPS = 2 * 3 * 512 * 1024 * 2048
+
+C1_FIRST = True
+WARM = 0
+
+
+def tile_nonlocalblocknd_pa_kernel(
+    tc, x_bytes, x_scale, g_w, g_b, theta_w, theta_b, phi_w, phi_b, out_0, out_1, out_2
+):
+    nc = tc.nc
+    weights = (theta_w, g_w, phi_w)
+    biases = (theta_b, g_b, phi_b)
+    outs = (out_1, out_0, out_2)
+
+    x_view = x_bytes[0].rearrange("(g p t) f h w -> p g t (f h w)", g=PASSES, p=P, t=PACK)
+    scale_view = x_scale[0, :, 0, 0, 0].rearrange("(g p t) -> p g t", g=PASSES, p=P, t=PACK)
+    w_view = [w.rearrange("(p m) k -> p m k", m=M_TILES) for w in weights]
+    b_view = [b.rearrange("(p m) -> p m", m=M_TILES) for b in biases]
+    out_view = [o[0].rearrange("(p m) n -> p m n", m=M_TILES) for o in outs]
+
+    with ExitStack() as ctx:
+        keep = ctx.enter_context(tc.tile_pool(name="keep", bufs=1))
+        theta_pool = ctx.enter_context(tc.tile_pool(name="theta_pool", bufs=6))
+        psum = ctx.enter_context(tc.psum_pool(name="psum", bufs=8))
+        ctx.enter_context(tc.manual_schedule())
+
+        ident = keep.tile([P, P], F32, name="ident")
+        x_scales = keep.tile([P, PASSES, PACK], F32, name="x_scales")
+        bias = keep.tile([P, 3, M_TILES], F32, name="bias")
+        warm = keep.tile([P, 2], F32, name="warm")
+        x_raw = [keep.tile([P, PASSES, PACK, CHUNK], U8, name="x_raw%d" % c) for c in range(CHUNKS)]
+        x_planes = [keep.tile([P, PASSES, PACK, CHUNK], BF16, name="x_planes%d" % c) for c in range(CHUNKS)]
+        mixed_pool = ctx.enter_context(tc.tile_pool(name="mixed_pool", bufs=1))
+        x_mixed = {}
+        x_codes = [keep.tile([P, PASSES, CHUNK], U32, name="x_codes%d" % c, align_bytes=64) for c in range(CHUNKS)]
+        x_blocks = [keep.tile([P, PASSES, CHUNK], U8, name="x_blocks%d" % c, align_bytes=64) for c in range(CHUNKS)]
+        w_raw = [keep.tile([P, 1024], BF16, name="w_raw%d" % j) for j in range(TILES)]
+        w_mixed = [keep.tile([P, 2 * 1024], BF16, name="w_mixed%d" % q, align_bytes=64) for q in range(TILES // 2)]
+        w_codes = [keep.tile([P, 2 * 256], U32, name="w_codes%d" % q, align_bytes=64) for q in range(TILES // 2)]
+        w_blocks = [keep.tile([P, 2 * 256], U8, name="w_blocks%d" % q, align_bytes=64) for q in range(TILES // 2)]
+        b_raw = [keep.tile([P, M_TILES], BF16, name="b_raw%d" % i) for i in range(3)]
+        pooled = keep.tile([P, 2, M_TILES, CHUNKS * POOLED], F32, name="pooled")
+        maxima = keep.tile([P, 2, M_TILES, CHUNKS * POOLED], F32, name="maxima")
+
+        banks = {}
+
+        def load_x(c):
+            for g in range(PASSES):
+                nc.sync.dma_start(out=x_raw[c][:, g, :, :], in_=x_view[:, g, :, c * CHUNK : (c + 1) * CHUNK])
+
+        def load_x_by_slot_pairs(c):
+            for g in range(PASSES):
+                for t in (2, 0):
+                    nc.sync.dma_start(
+                        out=x_raw[c][:, g, t : t + 2, :], in_=x_view[:, g, t : t + 2, c * CHUNK : (c + 1) * CHUNK]
+                    )
+
+        def load_w(j):
+            nc.sync.dma_start(out=w_raw[j][:], in_=w_view[j % 3][:, j // 3, :])
+
+        def load_biases():
+            for i in range(3):
+                nc.sync.dma_start(out=b_raw[i][:], in_=b_view[i])
+            for i in range(3):
+                nc.gpsimd.tensor_copy(out=bias[:, i, :], in_=b_raw[i][:])
+
+        def widen(c, g, t, engine):
+            codes = x_raw[c][:, g, t, :].bitcast(FP8)
+            if engine == "scalar":
+                nc.scalar.activation(out=x_planes[c][:, g, t, :], in_=codes, func=ACT.Copy, scale=x_scales[:, g, t : t + 1])
+            else:
+                nc.vector.tensor_scalar(
+                    out=x_planes[c][:, g, t, :], in0=codes, scalar1=x_scales[:, g, t : t + 1], scalar2=None, op0=ALU.mult
+                )
+
+        def interleave(c, g, engine):
+            if c not in x_mixed:
+                x_mixed[c] = mixed_pool.tile(
+                    [P, PASSES, PACK * CHUNK],
+                    BF16,
+                    tag=("mixed_first" if c == 0 else "mixed_rest"),
+                    name="x_mixed%d" % c,
+                    align_bytes=64,
+                )
+            pieces = 1 if engine == "vector" else HALVES
+            width = CHUNK // pieces
+            for h in range(pieces):
+                dst = x_mixed[c][:, g, PACK * h * width : PACK * (h + 1) * width].rearrange("p (n t) -> p n t", t=PACK)
+                src = x_planes[c][:, g, :, h * width : (h + 1) * width].rearrange("p t n -> p n t")
+                if engine == "vector":
+                    nc.vector.tensor_copy(out=dst, in_=src)
+                else:
+                    nc.gpsimd.tensor_scalar(out=dst, in0=src, scalar1=1.0, scalar2=0.0, op0=ALU.mult, op1=ALU.add)
+
+        def quantize_x(c):
+            nc.vector.quantize_mx(
+                out=x_codes[c][:].rearrange("p g n -> p (g n)").bitcast(FP8X4),
+                scales=x_blocks[c][:].rearrange("p g n -> p (g n)"),
+                in_=x_mixed[c][:].rearrange("p g n -> p (g n)"),
+            )
+
+        def transpose_w(j):
+            bank = psum.tile([P, PASSES, 2, P], F32, tag="bank", name="w_bank%d" % j)
+            banks["w", j] = bank
+            words = w_raw[j][:].bitcast(F32)
+            for g in range(PASSES):
+                for u in range(2):
+                    nc.tensor.transpose(bank[:, g, u, :], words[:, 256 * g + u : 256 * (g + 1) : 2], ident[:])
+
+        def copy_w(j, engine):
+            half = j % 2
+            dst = w_mixed[j // 2][:, half * 1024 : (half + 1) * 1024].bitcast(F32)
+            dst = dst.rearrange("p (g r u) -> p g r u", g=PASSES, u=2)
+            src = banks["w", j][:].rearrange("p g u r -> p g r u")
+            if engine == "scalar":
+                nc.scalar.copy(out=dst, in_=src)
+            else:
+                nc.vector.tensor_copy(out=dst, in_=src)
+
+        def quantize_w(q):
+            nc.vector.quantize_mx(out=w_codes[q][:].bitcast(FP8X4), scales=w_blocks[q][:], in_=w_mixed[q][:])
+
+        def multiply(j, c):
+            acc = psum.tile([P, CHUNK], F32, tag="bank", name="acc%d_%d" % (j, c))
+            banks[j, c] = acc
+            for g in range(PASSES):
+                w_cols = slice((j % 2) * 256 + g * P, (j % 2) * 256 + (g + 1) * P)
+                nc.tensor.matmul_mx(
+                    out=acc[:],
+                    lhsT=w_codes[j // 2][:, w_cols].bitcast(FP8X4),
+                    lhsT_scale=w_blocks[j // 2][:, w_cols],
+                    rhs=x_codes[c][:, g, :].bitcast(FP8X4),
+                    rhs_scale=x_blocks[c][:, g, :],
+                    start=(g == 0),
+                    stop=(g == PASSES - 1),
+                )
+
+        def finish_theta(m, c):
+            j = 3 * m + THETA
+            values = theta_pool.tile([P, CHUNK], F32, tag="theta", name="theta%d_%d" % (j, c))
+            nc.scalar.activation(
+                out=values[:], in_=banks[j, c][:], func=ACT.Identity, bias=bias[:, THETA, m : m + 1], scale=1.0
+            )
+            nc.sync.dma_start(out=out_view[THETA][:, m, c * CHUNK : (c + 1) * CHUNK], in_=values[:])
+
+        def pool(conv, m, c):
+            nc.vector.tensor_reduce(
+                out=maxima[:, conv - 1, m, c * POOLED : (c + 1) * POOLED].rearrange("p (a v) -> p a v", v=8),
+                in_=banks[3 * m + conv, c][:].rearrange("p (a h v w) -> p a v h w", h=2, v=8, w=2),
+                axis=AX.XY,
+                op=ALU.max,
+            )
+
+        def add_pool_bias(conv, m, first, last, engine):
+            cols = slice(first * POOLED, (last + 1) * POOLED)
+            column = bias[:, conv, m : m + 1]
+            if engine == "scalar":
+                nc.scalar.activation(
+                    out=pooled[:, conv - 1, m, cols], in_=maxima[:, conv - 1, m, cols], func=ACT.Identity, bias=column, scale=1.0
+                )
+            else:
+                nc.gpsimd.tensor_scalar(
+                    out=pooled[:, conv - 1, m, cols],
+                    in0=maxima[:, conv - 1, m, cols],
+                    scalar1=1.0,
+                    scalar2=column,
+                    op0=ALU.mult,
+                    op1=ALU.add,
+                )
+
+        def store_pooled(conv, first, last):
+            cols = slice(first * POOLED, (last + 1) * POOLED)
+            nc.sync.dma_start(out=out_view[conv][:, :, cols], in_=pooled[:, conv - 1, :, cols])
+
+        nc.gpsimd.memset(warm[:], 0.0)
+        nc.scalar.activation(out=warm[:, 1:2], in_=warm[:, 0:1], func=ACT.Copy, scale=1.0)
+        make_identity(nc, ident[:])
+
+        nc.sync.dma_start(out=x_scales[:], in_=scale_view)
+        load_x_by_slot_pairs(0)
+        for j in range(0, RUN):
+            load_w(j)
+        load_x(1)
+        load_biases()
+        for j in range(RUN, 2 * RUN):
+            load_w(j)
+        load_x(2)
+        for j in range(2 * RUN, TILES):
+            load_w(j)
+        load_x(3)
+
+        for g in range(PASSES):
+            widen(0, g, 2, "vector")
+            widen(0, g, 3, "vector")
+            widen(0, g, 0, "scalar")
+            widen(0, g, 1, "scalar")
+        for j in range(RUN):
+            transpose_w(j)
+        for j in range(RUN):
+            copy_w(j, "scalar")
+        for g in range(PASSES):
+            interleave(0, g, "vector")
+        quantize_x(0)
+        for q in range(RUN // 2):
+            quantize_w(q)
+        for g in range(PASSES):
+            for t in range(PACK):
+                widen(1, g, t, "scalar")
+            interleave(1, g, "gpsimd")
+        for c in range(CHUNKS):
+            for m in range(M_TILES):
+                last_triple = c == CHUNKS - 1 and m == M_TILES - 1
+                if not last_triple:
+                    multiply(3 * m + THETA, c)
+                    finish_theta(m, c)
+                if c + 2 < CHUNKS:
+                    for plane in (2 * m, 2 * m + 1):
+                        widen(c + 2, plane // PACK, plane % PACK, "scalar")
+                elif c == CHUNKS - 2:
+                    for conv in (G, PHI):
+                        add_pool_bias(conv, m, 0, 1, "scalar")
+                    if m == M_TILES - 1:
+                        for conv in (G, PHI):
+                            store_pooled(conv, 0, 1)
+                elif m < 2:
+                    for tile in (2 * m, 2 * m + 1):
+                        for conv in (G, PHI):
+                            add_pool_bias(conv, tile, 2, 2, "scalar")
+                    if m == 1:
+                        for conv in (G, PHI):
+                            store_pooled(conv, 2, 2)
+                for conv in (G, PHI):
+                    multiply(3 * m + conv, c)
+                    pool(conv, m, c)
+                    if c == CHUNKS - 1:
+                        add_pool_bias(conv, m, c, c, "gpsimd")
+                if last_triple:
+                    for conv in (G, PHI):
+                        store_pooled(conv, c, c)
+                    multiply(3 * m + THETA, c)
+                    finish_theta(m, c)
+                if c == 0 and m == 0:
+                    for j in range(RUN, 2 * RUN):
+                        transpose_w(j)
+                    for j in range(RUN, 2 * RUN):
+                        copy_w(j, "vector")
+                        if j % 2 == 1:
+                            quantize_w(j // 2)
+                if c == 0 and m == 1:
+                    for j in range(2 * RUN, TILES):
+                        transpose_w(j)
+                    for j in range(2 * RUN, TILES):
+                        copy_w(j, "scalar")
+                    if C1_FIRST:
+                        quantize_x(1)
+                    for q in range(RUN, TILES // 2):
+                        quantize_w(q)
+                if m == 1 and c + 1 < CHUNKS and not (c == 0 and C1_FIRST):
+                    quantize_x(c + 1)
+                if m in (1, 3) and c + 2 < CHUNKS:
+                    interleave(c + 2, m // 2, "gpsimd")

@@ -112,8 +112,8 @@ def tile_nonlocalblocknd_pa_kernel(
             pieces = 1 if engine == "vector" else HALVES
             width = CHUNK // pieces
             for h in range(pieces):
-                dst = x_mixed[c][:, g, PACK * h * width : PACK * (h + 1) * width].rearrange("p (n t) -> p n t", t=PACK)
-                src = x_planes[c][:, g, :, h * width : (h + 1) * width].rearrange("p t n -> p n t")
+                dst = x_mixed[c][:, g, PACK * h * width : PACK * (h + 1) * width].rearrange("p (n i t) -> p n t i", i=4, t=PACK)
+                src = x_planes[c][:, g, :, h * width : (h + 1) * width].rearrange("p t (n i) -> p n t i", i=4)
                 if engine == "vector":
                     nc.vector.tensor_copy(out=dst, in_=src)
                 else:

@@ -112,11 +112,15 @@ def tile_nonlocalblocknd_pa_kernel(
             pieces = 1 if engine == "vector" else HALVES
             width = CHUNK // pieces
             for h in range(pieces):
-                dst = x_mixed[c][:, g, PACK * h * width : PACK * (h + 1) * width].rearrange("p (n i t) -> p n t i", i=4, t=PACK)
-                src = x_planes[c][:, g, :, h * width : (h + 1) * width].rearrange("p t (n i) -> p n t i", i=4)
+                mixed = x_mixed[c][:, g, PACK * h * width : PACK * (h + 1) * width]
+                planes = x_planes[c][:, g, :, h * width : (h + 1) * width]
                 if engine == "vector":
-                    nc.vector.tensor_copy(out=dst, in_=src)
+                    nc.vector.tensor_copy(
+                        out=mixed.rearrange("p (n i t) -> p n t i", i=4, t=PACK), in_=planes.rearrange("p t (n i) -> p n t i", i=4)
+                    )
                 else:
+                    dst = mixed.rearrange("p (n t) -> p n t", t=PACK)
+                    src = planes.rearrange("p t n -> p n t")
                     nc.gpsimd.tensor_scalar(out=dst, in0=src, scalar1=1.0, scalar2=0.0, op0=ALU.mult, op1=ALU.add)
 
         def quantize_x(c):

@@ -87,7 +87,7 @@ def tile_nonlocalblocknd_pa_kernel(
 
         def load_biases():
             for i in range(3):
-                nc.sync.dma_start(out=b_raw[i][:], in_=b_view[i])
+                nc.scalar.dma_start(out=b_raw[i][:], in_=b_view[i])
             for i in range(3):
                 nc.gpsimd.tensor_copy(out=bias[:, i, :], in_=b_raw[i][:])
 
@@ -100,7 +100,7 @@ def tile_nonlocalblocknd_pa_kernel(
                     out=x_planes[c][:, g, t, :], in0=codes, scalar1=x_scales[:, g, t : t + 1], scalar2=None, op0=ALU.mult
                 )
 
-        def interleave(c, g, engine):
+        def interleave(c, g, engine, first=0, last=HALVES):
             if c not in x_mixed:
                 x_mixed[c] = mixed_pool.tile(
                     [P, PASSES, PACK * CHUNK],
@@ -109,19 +109,21 @@ def tile_nonlocalblocknd_pa_kernel(
                     name="x_mixed%d" % c,
                     align_bytes=64,
                 )
-            pieces = 1 if engine == "vector" else HALVES
-            width = CHUNK // pieces
-            for h in range(pieces):
-                mixed = x_mixed[c][:, g, PACK * h * width : PACK * (h + 1) * width]
-                planes = x_planes[c][:, g, :, h * width : (h + 1) * width]
-                if engine == "vector":
-                    nc.vector.tensor_copy(
-                        out=mixed.rearrange("p (n i t) -> p n t i", i=4, t=PACK), in_=planes.rearrange("p t (n i) -> p n t i", i=4)
-                    )
-                else:
-                    dst = mixed.rearrange("p (n t) -> p n t", t=PACK)
-                    src = planes.rearrange("p t n -> p n t")
+            width = CHUNK // HALVES
+            if engine == "vector":
+                mixed = x_mixed[c][:, g, PACK * first * width : PACK * last * width]
+                planes = x_planes[c][:, g, :, first * width : last * width]
+                nc.vector.tensor_copy(
+                    out=mixed.rearrange("p (n i t) -> p n t i", i=4, t=PACK), in_=planes.rearrange("p t (n i) -> p n t i", i=4)
+                )
+            else:
+                for h in range(first, last):
+                    dst = x_mixed[c][:, g, PACK * h * width : PACK * (h + 1) * width].rearrange("p (n t) -> p n t", t=PACK)
+                    src = x_planes[c][:, g, :, h * width : (h + 1) * width].rearrange("p t n -> p n t")
                     nc.gpsimd.tensor_scalar(out=dst, in0=src, scalar1=1.0, scalar2=0.0, op0=ALU.mult, op1=ALU.add)
+
+        def gpsimd_share(c, g):
+            interleave(c, g, "gpsimd", 0, HALVES - g)
 
         def quantize_x(c):
             nc.vector.quantize_mx(
@@ -206,18 +208,16 @@ def tile_nonlocalblocknd_pa_kernel(
         nc.gpsimd.memset(warm[:], 0.0)
         nc.scalar.activation(out=warm[:, 1:2], in_=warm[:, 0:1], func=ACT.Copy, scale=1.0)
         make_identity(nc, ident[:])
+        load_biases()
 
         nc.sync.dma_start(out=x_scales[:], in_=scale_view)
         load_x_by_slot_pairs(0)
-        for j in range(0, RUN):
+        for j in range(0, 2 * RUN):
             load_w(j)
         load_x(1)
-        load_biases()
-        for j in range(RUN, 2 * RUN):
-            load_w(j)
-        load_x(2)
         for j in range(2 * RUN, TILES):
             load_w(j)
+        load_x(2)
         load_x(3)
 
         for g in range(PASSES):
@@ -225,26 +225,37 @@ def tile_nonlocalblocknd_pa_kernel(
             widen(0, g, 3, "vector")
             widen(0, g, 0, "scalar")
             widen(0, g, 1, "scalar")
-        for j in range(RUN):
+        for j in range(2 * RUN):
             transpose_w(j)
-        for j in range(RUN):
+        for j in range(2 * RUN):
             copy_w(j, "scalar")
         for g in range(PASSES):
             interleave(0, g, "vector")
         quantize_x(0)
-        for q in range(RUN // 2):
-            quantize_w(q)
-        for g in range(PASSES):
-            for t in range(PACK):
-                widen(1, g, t, "scalar")
-            interleave(1, g, "gpsimd")
+        quantize_w(0)
+        quantize_w(1)
+        for t in range(PACK):
+            widen(1, 0, t, "vector")
+        interleave(1, 0, "gpsimd")
+        quantize_w(2)
+        quantize_w(3)
         for c in range(CHUNKS):
             for m in range(M_TILES):
                 last_triple = c == CHUNKS - 1 and m == M_TILES - 1
                 if not last_triple:
                     multiply(3 * m + THETA, c)
                     finish_theta(m, c)
-                if c + 2 < CHUNKS:
+                if c == 0 and m == 0:
+                    for t in range(PACK):
+                        widen(1, 1, t, "scalar")
+                    interleave(1, 1, "gpsimd")
+                elif c == 0 and m >= 2:
+                    if m == 2:
+                        quantize_x(1)
+                    for t in range(PACK):
+                        widen(2, m - 2, t, "scalar")
+                    gpsimd_share(2, m - 2)
+                elif 0 < c and c + 2 < CHUNKS:
                     for plane in (2 * m, 2 * m + 1):
                         widen(c + 2, plane // PACK, plane % PACK, "scalar")
                 elif c == CHUNKS - 2:
@@ -253,13 +264,15 @@ def tile_nonlocalblocknd_pa_kernel(
                     if m == M_TILES - 1:
                         for conv in (G, PHI):
                             store_pooled(conv, 0, 1)
-                elif m < 2:
+                elif c == CHUNKS - 1 and m < 2:
                     for tile in (2 * m, 2 * m + 1):
                         for conv in (G, PHI):
                             add_pool_bias(conv, tile, 2, 2, "scalar")
                     if m == 1:
                         for conv in (G, PHI):
                             store_pooled(conv, 2, 2)
+                if m == 1 and 0 < c and c + 1 < CHUNKS:
+                    interleave(c + 1, 1, "vector", 1, 2)
                 for conv in (G, PHI):
                     multiply(3 * m + conv, c)
                     pool(conv, m, c)
@@ -270,23 +283,14 @@ def tile_nonlocalblocknd_pa_kernel(
                         store_pooled(conv, c, c)
                     multiply(3 * m + THETA, c)
                     finish_theta(m, c)
-                if c == 0 and m == 0:
-                    for j in range(RUN, 2 * RUN):
-                        transpose_w(j)
-                    for j in range(RUN, 2 * RUN):
-                        copy_w(j, "vector")
-                        if j % 2 == 1:
-                            quantize_w(j // 2)
                 if c == 0 and m == 1:
                     for j in range(2 * RUN, TILES):
                         transpose_w(j)
                     for j in range(2 * RUN, TILES):
                         copy_w(j, "scalar")
-                    if C1_FIRST:
-                        quantize_x(1)
-                    for q in range(RUN, TILES // 2):
-                        quantize_w(q)
-                if m == 1 and c + 1 < CHUNKS and not (c == 0 and C1_FIRST):
+                        if j % 2 == 1:
+                            quantize_w(j // 2)
+                if m == 1 and 0 < c and c + 1 < CHUNKS:
                     quantize_x(c + 1)
-                if m in (1, 3) and c + 2 < CHUNKS:
-                    interleave(c + 2, m // 2, "gpsimd")
+                if m in (1, 3) and 0 < c and c + 2 < CHUNKS:
+                    gpsimd_share(c + 2, m // 2)

@@ -87,7 +87,7 @@ def tile_nonlocalblocknd_pa_kernel(
 
         def load_biases():
             for i in range(3):
-                nc.scalar.dma_start(out=b_raw[i][:], in_=b_view[i])
+                nc.sync.dma_start(out=b_raw[i][:], in_=b_view[i])
             for i in range(3):
                 nc.gpsimd.tensor_copy(out=bias[:, i, :], in_=b_raw[i][:])
 
@@ -172,7 +172,7 @@ def tile_nonlocalblocknd_pa_kernel(
             j = 3 * m + THETA
             values = theta_pool.tile([P, CHUNK], F32, tag="theta", name="theta%d_%d" % (j, c))
             nc.scalar.activation(
-                out=values[:], in_=banks[j, c][:], func=ACT.Identity, bias=bias[:, THETA, m : m + 1], scale=1.0
+                out=values[:], in_=banks[j, c][:], func=ACT.Identity, bias=b_raw[THETA][:, m : m + 1], scale=1.0
             )
             nc.sync.dma_start(out=out_view[THETA][:, m, c * CHUNK : (c + 1) * CHUNK], in_=values[:])
 
@@ -208,12 +208,12 @@ def tile_nonlocalblocknd_pa_kernel(
         nc.gpsimd.memset(warm[:], 0.0)
         nc.scalar.activation(out=warm[:, 1:2], in_=warm[:, 0:1], func=ACT.Copy, scale=1.0)
         make_identity(nc, ident[:])
-        load_biases()
 
         nc.sync.dma_start(out=x_scales[:], in_=scale_view)
         load_x_by_slot_pairs(0)
         for j in range(0, 2 * RUN):
             load_w(j)
+        load_biases()
         load_x(1)
         for j in range(2 * RUN, TILES):
             load_w(j)
@@ -232,13 +232,11 @@ def tile_nonlocalblocknd_pa_kernel(
         for g in range(PASSES):
             interleave(0, g, "vector")
         quantize_x(0)
-        quantize_w(0)
-        quantize_w(1)
+        for q in range(RUN):
+            quantize_w(q)
         for t in range(PACK):
             widen(1, 0, t, "vector")
-        interleave(1, 0, "gpsimd")
-        quantize_w(2)
-        quantize_w(3)
+        gpsimd_share(1, 0)
         for c in range(CHUNKS):
             for m in range(M_TILES):
                 last_triple = c == CHUNKS - 1 and m == M_TILES - 1
@@ -248,7 +246,7 @@ def tile_nonlocalblocknd_pa_kernel(
                 if c == 0 and m == 0:
                     for t in range(PACK):
                         widen(1, 1, t, "scalar")
-                    interleave(1, 1, "gpsimd")
+                    gpsimd_share(1, 1)
                 elif c == 0 and m >= 2:
                     if m == 2:
                         quantize_x(1)
@@ -286,6 +284,7 @@ def tile_nonlocalblocknd_pa_kernel(
                 if c == 0 and m == 1:
                     for j in range(2 * RUN, TILES):
                         transpose_w(j)
+                    interleave(1, 1, "vector", 1, 2)
                     for j in range(2 * RUN, TILES):
                         copy_w(j, "scalar")
                         if j % 2 == 1:

@@ -76,8 +76,8 @@ def tile_nonlocalblocknd_pa_kernel(
                 nc.sync.dma_start(out=x_raw[c][:, g, :, :], in_=x_view[:, g, :, c * CHUNK : (c + 1) * CHUNK])
 
         def load_x_by_slot_pairs(c):
-            for g in range(PASSES):
-                for t in (2, 0):
+            for g, pairs in ((0, (2, 0)), (1, (0, 2))):
+                for t in pairs:
                     nc.sync.dma_start(
                         out=x_raw[c][:, g, t : t + 2, :], in_=x_view[:, g, t : t + 2, c * CHUNK : (c + 1) * CHUNK]
                     )
@@ -153,6 +153,14 @@ def tile_nonlocalblocknd_pa_kernel(
         def quantize_w(q):
             nc.vector.quantize_mx(out=w_codes[q][:].bitcast(FP8X4), scales=w_blocks[q][:], in_=w_mixed[q][:])
 
+        def quantize_w_tile(j):
+            half = j % 2
+            nc.vector.quantize_mx(
+                out=w_codes[j // 2][:, half * 256 : (half + 1) * 256].bitcast(FP8X4),
+                scales=w_blocks[j // 2][:, half * 256 : (half + 1) * 256],
+                in_=w_mixed[j // 2][:, half * 1024 : (half + 1) * 1024],
+            )
+
         def multiply(j, c):
             acc = psum.tile([P, CHUNK], F32, tag="bank", name="acc%d_%d" % (j, c))
             banks[j, c] = acc
@@ -220,19 +228,22 @@ def tile_nonlocalblocknd_pa_kernel(
         load_x(2)
         load_x(3)
 
-        for g in range(PASSES):
-            widen(0, g, 2, "vector")
-            widen(0, g, 3, "vector")
-            widen(0, g, 0, "scalar")
-            widen(0, g, 1, "scalar")
+        for t in (2, 3, 1):
+            widen(0, 0, t, "vector")
+        widen(0, 1, 1, "vector")
+        widen(0, 0, 0, "scalar")
+        for t in (0, 2, 3):
+            widen(0, 1, t, "scalar")
         for j in range(2 * RUN):
             transpose_w(j)
         for j in range(2 * RUN):
             copy_w(j, "scalar")
         for g in range(PASSES):
             interleave(0, g, "vector")
+        quantize_w_tile(0)
         quantize_x(0)
-        for q in range(RUN):
+        quantize_w_tile(1)
+        for q in range(1, RUN):
             quantize_w(q)
         for t in range(PACK):
             widen(1, 0, t, "vector")

@@ -257,7 +257,6 @@ def tile_nonlocalblocknd_pa_kernel(
                 if c == 0 and m == 0:
                     for t in range(PACK):
                         widen(1, 1, t, "scalar")
-                    gpsimd_share(1, 1)
                 elif c == 0 and m >= 2:
                     if m == 2:
                         quantize_x(1)
@@ -295,7 +294,7 @@ def tile_nonlocalblocknd_pa_kernel(
                 if c == 0 and m == 1:
                     for j in range(2 * RUN, TILES):
                         transpose_w(j)
-                    interleave(1, 1, "vector", 1, 2)
+                    interleave(1, 1, "vector")
                     for j in range(2 * RUN, TILES):
                         copy_w(j, "scalar")
                         if j % 2 == 1:

@@ -85,11 +85,12 @@ def tile_nonlocalblocknd_pa_kernel(
         def load_w(j):
             nc.sync.dma_start(out=w_raw[j][:], in_=w_view[j % 3][:, j // 3, :])
 
-        def load_biases():
-            for i in range(3):
-                nc.sync.dma_start(out=b_raw[i][:], in_=b_view[i])
-            for i in range(3):
-                nc.gpsimd.tensor_copy(out=bias[:, i, :], in_=b_raw[i][:])
+        def load_bias(conv):
+            nc.sync.dma_start(out=b_raw[conv][:], in_=b_view[conv])
+
+        def widen_pool_biases():
+            for conv in (G, PHI):
+                nc.gpsimd.tensor_copy(out=bias[:, conv, :], in_=b_raw[conv][:])
 
         def widen(c, g, t, engine):
             codes = x_raw[c][:, g, t, :].bitcast(FP8)
@@ -221,10 +222,12 @@ def tile_nonlocalblocknd_pa_kernel(
         load_x_by_slot_pairs(0)
         for j in range(0, 2 * RUN):
             load_w(j)
-        load_biases()
+        load_bias(THETA)
         load_x(1)
         for j in range(2 * RUN, TILES):
             load_w(j)
+        for conv in (G, PHI):
+            load_bias(conv)
         load_x(2)
         load_x(3)
 
@@ -243,11 +246,13 @@ def tile_nonlocalblocknd_pa_kernel(
         quantize_w_tile(0)
         quantize_x(0)
         quantize_w_tile(1)
-        for q in range(1, RUN):
+        for q in range(1, RUN - 1):
             quantize_w(q)
         for t in range(PACK):
             widen(1, 0, t, "vector")
+        quantize_w(RUN - 1)
         gpsimd_share(1, 0)
+        widen_pool_biases()
         for c in range(CHUNKS):
             for m in range(M_TILES):
                 last_triple = c == CHUNKS - 1 and m == M_TILES - 1

@@ -255,10 +255,8 @@ def tile_nonlocalblocknd_pa_kernel(
         widen_pool_biases()
         for c in range(CHUNKS):
             for m in range(M_TILES):
-                last_triple = c == CHUNKS - 1 and m == M_TILES - 1
-                if not last_triple:
-                    multiply(3 * m + THETA, c)
-                    finish_theta(m, c)
+                multiply(3 * m + THETA, c)
+                finish_theta(m, c)
                 if c == 0 and m == 0:
                     for t in range(PACK):
                         widen(1, 1, t, "scalar")
@@ -286,16 +284,18 @@ def tile_nonlocalblocknd_pa_kernel(
                             store_pooled(conv, 2, 2)
                 if m == 1 and 0 < c and c + 1 < CHUNKS:
                     interleave(c + 1, 1, "vector", 1, 2)
-                for conv in (G, PHI):
-                    multiply(3 * m + conv, c)
-                    pool(conv, m, c)
+                if c < CHUNKS - 1:
+                    pair = ((G, m), (PHI, m))
+                else:
+                    conv = G if m < 2 else PHI
+                    pair = ((conv, 2 * m % M_TILES), (conv, 2 * m % M_TILES + 1))
+                for conv, tile in pair:
+                    multiply(3 * tile + conv, c)
+                    pool(conv, tile, c)
                     if c == CHUNKS - 1:
-                        add_pool_bias(conv, m, c, c, "gpsimd")
-                if last_triple:
-                    for conv in (G, PHI):
-                        store_pooled(conv, c, c)
-                    multiply(3 * m + THETA, c)
-                    finish_theta(m, c)
+                        add_pool_bias(conv, tile, c, c, "gpsimd")
+                if c == CHUNKS - 1 and m in (1, 3):
+                    store_pooled(G if m == 1 else PHI, c, c)
                 if c == 0 and m == 1:
                     for j in range(2 * RUN, TILES):
                         transpose_w(j)

@@ -123,9 +123,6 @@ def tile_nonlocalblocknd_pa_kernel(
                     src = x_planes[c][:, g, :, h * width : (h + 1) * width].rearrange("p t n -> p n t")
                     nc.gpsimd.tensor_scalar(out=dst, in0=src, scalar1=1.0, scalar2=0.0, op0=ALU.mult, op1=ALU.add)
 
-        def gpsimd_share(c, g):
-            interleave(c, g, "gpsimd", 0, HALVES - g)
-
         def quantize_x(c):
             nc.vector.quantize_mx(
                 out=x_codes[c][:].rearrange("p g n -> p (g n)").bitcast(FP8X4),
@@ -214,11 +211,11 @@ def tile_nonlocalblocknd_pa_kernel(
             cols = slice(first * POOLED, (last + 1) * POOLED)
             nc.sync.dma_start(out=out_view[conv][:, :, cols], in_=pooled[:, conv - 1, :, cols])
 
+        nc.scalar.dma_start(out=x_scales[:], in_=scale_view)
         nc.gpsimd.memset(warm[:], 0.0)
         nc.scalar.activation(out=warm[:, 1:2], in_=warm[:, 0:1], func=ACT.Copy, scale=1.0)
         make_identity(nc, ident[:])
 
-        nc.sync.dma_start(out=x_scales[:], in_=scale_view)
         load_x_by_slot_pairs(0)
         for j in range(0, 2 * RUN):
             load_w(j)
@@ -251,7 +248,7 @@ def tile_nonlocalblocknd_pa_kernel(
         for t in range(PACK):
             widen(1, 0, t, "vector")
         quantize_w(RUN - 1)
-        gpsimd_share(1, 0)
+        interleave(1, 0, "gpsimd")
         widen_pool_biases()
         for c in range(CHUNKS):
             for m in range(M_TILES):
@@ -265,7 +262,8 @@ def tile_nonlocalblocknd_pa_kernel(
                         quantize_x(1)
                     for t in range(PACK):
                         widen(2, m - 2, t, "scalar")
-                    gpsimd_share(2, m - 2)
+                    if m == 2:
+                        interleave(2, 0, "gpsimd")
                 elif 0 < c and c + 2 < CHUNKS:
                     for plane in (2 * m, 2 * m + 1):
                         widen(c + 2, plane // PACK, plane % PACK, "scalar")
@@ -283,7 +281,7 @@ def tile_nonlocalblocknd_pa_kernel(
                         for conv in (G, PHI):
                             store_pooled(conv, 2, 2)
                 if m == 1 and 0 < c and c + 1 < CHUNKS:
-                    interleave(c + 1, 1, "vector", 1, 2)
+                    interleave(c + 1, 1, "vector")
                 if c < CHUNKS - 1:
                     pair = ((G, m), (PHI, m))
                 else:
@@ -292,13 +290,16 @@ def tile_nonlocalblocknd_pa_kernel(
                 for conv, tile in pair:
                     multiply(3 * tile + conv, c)
                     pool(conv, tile, c)
+                    if c == 0 and m == 1:
+                        half = RUN // 2
+                        first = 2 * RUN + (0 if conv == G else half)
+                        for j in range(first, first + half):
+                            transpose_w(j)
                     if c == CHUNKS - 1:
                         add_pool_bias(conv, tile, c, c, "gpsimd")
                 if c == CHUNKS - 1 and m in (1, 3):
                     store_pooled(G if m == 1 else PHI, c, c)
                 if c == 0 and m == 1:
-                    for j in range(2 * RUN, TILES):
-                        transpose_w(j)
                     interleave(1, 1, "vector")
                     for j in range(2 * RUN, TILES):
                         copy_w(j, "scalar")
@@ -306,5 +307,5 @@ def tile_nonlocalblocknd_pa_kernel(
                             quantize_w(j // 2)
                 if m == 1 and 0 < c and c + 1 < CHUNKS:
                     quantize_x(c + 1)
-                if m in (1, 3) and 0 < c and c + 2 < CHUNKS:
-                    gpsimd_share(c + 2, m // 2)
+                if m == 1 and 0 < c and c + 2 < CHUNKS:
+                    interleave(c + 2, 0, "gpsimd")

from contextlib import ExitStack

import concourse.mybir as mybir
from concourse.masks import make_identity

F32 = mybir.dt.float32
BF16 = mybir.dt.bfloat16
U32 = mybir.dt.uint32
U8 = mybir.dt.uint8
FP8 = mybir.dt.float8_e4m3fn
FP8X4 = mybir.dt.float8_e4m3fn_x4
ACT = mybir.ActivationFunctionType
ALU = mybir.AluOpType
AX = mybir.AxisListType

P = 128
PACK = 4
PASSES = 2
CHUNK = 512
CHUNKS = 4
POOLED = CHUNK // 4
M_TILES = 4
TILES = 3 * M_TILES
THETA, G, PHI = 0, 1, 2
RUN = 4
HALVES = 2

FLOPS = 2 * 3 * 512 * 1024 * 2048

C1_FIRST = True
WARM = 0


def tile_nonlocalblocknd_pa_kernel(
    tc, x_bytes, x_scale, g_w, g_b, theta_w, theta_b, phi_w, phi_b, out_0, out_1, out_2
):
    nc = tc.nc
    weights = (theta_w, g_w, phi_w)
    biases = (theta_b, g_b, phi_b)
    outs = (out_1, out_0, out_2)

    x_view = x_bytes[0].rearrange("(g p t) f h w -> p g t (f h w)", g=PASSES, p=P, t=PACK)
    scale_view = x_scale[0, :, 0, 0, 0].rearrange("(g p t) -> p g t", g=PASSES, p=P, t=PACK)
    w_view = [w.rearrange("(p m) k -> p m k", m=M_TILES) for w in weights]
    b_view = [b.rearrange("(p m) -> p m", m=M_TILES) for b in biases]
    out_view = [o[0].rearrange("(p m) n -> p m n", m=M_TILES) for o in outs]

    with ExitStack() as ctx:
        keep = ctx.enter_context(tc.tile_pool(name="keep", bufs=1))
        theta_pool = ctx.enter_context(tc.tile_pool(name="theta_pool", bufs=6))
        psum = ctx.enter_context(tc.psum_pool(name="psum", bufs=8))
        ctx.enter_context(tc.manual_schedule())

        ident = keep.tile([P, P], F32, name="ident")
        x_scales = keep.tile([P, PASSES, PACK], F32, name="x_scales")
        bias = keep.tile([P, 3, M_TILES], F32, name="bias")
        warm = keep.tile([P, 2], F32, name="warm")
        x_raw = [keep.tile([P, PASSES, PACK, CHUNK], U8, name="x_raw%d" % c) for c in range(CHUNKS)]
        x_planes = [keep.tile([P, PASSES, PACK, CHUNK], BF16, name="x_planes%d" % c) for c in range(CHUNKS)]
        mixed_pool = ctx.enter_context(tc.tile_pool(name="mixed_pool", bufs=1))
        x_mixed = {}
        x_codes = [keep.tile([P, PASSES, CHUNK], U32, name="x_codes%d" % c, align_bytes=64) for c in range(CHUNKS)]
        x_blocks = [keep.tile([P, PASSES, CHUNK], U8, name="x_blocks%d" % c, align_bytes=64) for c in range(CHUNKS)]
        w_raw = [keep.tile([P, 1024], BF16, name="w_raw%d" % j) for j in range(TILES)]
        w_mixed = [keep.tile([P, 2 * 1024], BF16, name="w_mixed%d" % q, align_bytes=64) for q in range(TILES // 2)]
        w_codes = [keep.tile([P, 2 * 256], U32, name="w_codes%d" % q, align_bytes=64) for q in range(TILES // 2)]
        w_blocks = [keep.tile([P, 2 * 256], U8, name="w_blocks%d" % q, align_bytes=64) for q in range(TILES // 2)]
        b_raw = [keep.tile([P, M_TILES], BF16, name="b_raw%d" % i) for i in range(3)]
        pooled = keep.tile([P, 2, M_TILES, CHUNKS * POOLED], F32, name="pooled")
        maxima = keep.tile([P, 2, M_TILES, CHUNKS * POOLED], F32, name="maxima")

        banks = {}

        def load_x(c):
            for g in range(PASSES):
                nc.sync.dma_start(out=x_raw[c][:, g, :, :], in_=x_view[:, g, :, c * CHUNK : (c + 1) * CHUNK])

        def load_x_by_slot_pairs(c):
            for g, pairs in ((0, (2, 0)), (1, (0, 2))):
                for t in pairs:
                    nc.sync.dma_start(
                        out=x_raw[c][:, g, t : t + 2, :], in_=x_view[:, g, t : t + 2, c * CHUNK : (c + 1) * CHUNK]
                    )

        def load_w(j):
            nc.sync.dma_start(out=w_raw[j][:], in_=w_view[j % 3][:, j // 3, :])

        def load_bias(conv):
            nc.sync.dma_start(out=b_raw[conv][:], in_=b_view[conv])

        def widen_pool_biases():
            for conv in (G, PHI):
                nc.gpsimd.tensor_copy(out=bias[:, conv, :], in_=b_raw[conv][:])

        def widen(c, g, t, engine):
            codes = x_raw[c][:, g, t, :].bitcast(FP8)
            if engine == "scalar":
                nc.scalar.activation(out=x_planes[c][:, g, t, :], in_=codes, func=ACT.Copy, scale=x_scales[:, g, t : t + 1])
            else:
                nc.vector.tensor_scalar(
                    out=x_planes[c][:, g, t, :], in0=codes, scalar1=x_scales[:, g, t : t + 1], scalar2=None, op0=ALU.mult
                )

        def interleave(c, g, engine, first=0, last=HALVES):
            if c not in x_mixed:
                x_mixed[c] = mixed_pool.tile(
                    [P, PASSES, PACK * CHUNK],
                    BF16,
                    tag=("mixed_first" if c == 0 else "mixed_rest"),
                    name="x_mixed%d" % c,
                    align_bytes=64,
                )
            width = CHUNK // HALVES
            if engine == "vector":
                mixed = x_mixed[c][:, g, PACK * first * width : PACK * last * width]
                planes = x_planes[c][:, g, :, first * width : last * width]
                nc.vector.tensor_copy(
                    out=mixed.rearrange("p (n i t) -> p n t i", i=4, t=PACK), in_=planes.rearrange("p t (n i) -> p n t i", i=4)
                )
            else:
                for h in range(first, last):
                    dst = x_mixed[c][:, g, PACK * h * width : PACK * (h + 1) * width].rearrange("p (n t) -> p n t", t=PACK)
                    src = x_planes[c][:, g, :, h * width : (h + 1) * width].rearrange("p t n -> p n t")
                    nc.gpsimd.tensor_scalar(out=dst, in0=src, scalar1=1.0, scalar2=0.0, op0=ALU.mult, op1=ALU.add)

        def quantize_x(c):
            nc.vector.quantize_mx(
                out=x_codes[c][:].rearrange("p g n -> p (g n)").bitcast(FP8X4),
                scales=x_blocks[c][:].rearrange("p g n -> p (g n)"),
                in_=x_mixed[c][:].rearrange("p g n -> p (g n)"),
            )

        def transpose_w(j):
            bank = psum.tile([P, PASSES, 2, P], F32, tag="bank", name="w_bank%d" % j)
            banks["w", j] = bank
            words = w_raw[j][:].bitcast(F32)
            for g in range(PASSES):
                for u in range(2):
                    nc.tensor.transpose(bank[:, g, u, :], words[:, 256 * g + u : 256 * (g + 1) : 2], ident[:])

        def copy_w(j, engine):
            half = j % 2
            dst = w_mixed[j // 2][:, half * 1024 : (half + 1) * 1024].bitcast(F32)
            dst = dst.rearrange("p (g r u) -> p g r u", g=PASSES, u=2)
            src = banks["w", j][:].rearrange("p g u r -> p g r u")
            if engine == "scalar":
                nc.scalar.copy(out=dst, in_=src)
            else:
                nc.vector.tensor_copy(out=dst, in_=src)

        def quantize_w(q):
            nc.vector.quantize_mx(out=w_codes[q][:].bitcast(FP8X4), scales=w_blocks[q][:], in_=w_mixed[q][:])

        def quantize_w_tile(j):
            half = j % 2
            nc.vector.quantize_mx(
                out=w_codes[j // 2][:, half * 256 : (half + 1) * 256].bitcast(FP8X4),
                scales=w_blocks[j // 2][:, half * 256 : (half + 1) * 256],
                in_=w_mixed[j // 2][:, half * 1024 : (half + 1) * 1024],
            )

        def multiply(j, c):
            acc = psum.tile([P, CHUNK], F32, tag="bank", name="acc%d_%d" % (j, c))
            banks[j, c] = acc
            for g in range(PASSES):
                w_cols = slice((j % 2) * 256 + g * P, (j % 2) * 256 + (g + 1) * P)
                nc.tensor.matmul_mx(
                    out=acc[:],
                    lhsT=w_codes[j // 2][:, w_cols].bitcast(FP8X4),
                    lhsT_scale=w_blocks[j // 2][:, w_cols],
                    rhs=x_codes[c][:, g, :].bitcast(FP8X4),
                    rhs_scale=x_blocks[c][:, g, :],
                    start=(g == 0),
                    stop=(g == PASSES - 1),
                )

        def finish_theta(m, c):
            j = 3 * m + THETA
            values = theta_pool.tile([P, CHUNK], F32, tag="theta", name="theta%d_%d" % (j, c))
            nc.scalar.activation(
                out=values[:], in_=banks[j, c][:], func=ACT.Identity, bias=b_raw[THETA][:, m : m + 1], scale=1.0
            )
            nc.sync.dma_start(out=out_view[THETA][:, m, c * CHUNK : (c + 1) * CHUNK], in_=values[:])

        def pool(conv, m, c):
            nc.vector.tensor_reduce(
                out=maxima[:, conv - 1, m, c * POOLED : (c + 1) * POOLED].rearrange("p (a v) -> p a v", v=8),
                in_=banks[3 * m + conv, c][:].rearrange("p (a h v w) -> p a v h w", h=2, v=8, w=2),
                axis=AX.XY,
                op=ALU.max,
            )

        def add_pool_bias(conv, m, first, last, engine):
            cols = slice(first * POOLED, (last + 1) * POOLED)
            column = bias[:, conv, m : m + 1]
            if engine == "scalar":
                nc.scalar.activation(
                    out=pooled[:, conv - 1, m, cols], in_=maxima[:, conv - 1, m, cols], func=ACT.Identity, bias=column, scale=1.0
                )
            else:
                nc.gpsimd.tensor_scalar(
                    out=pooled[:, conv - 1, m, cols],
                    in0=maxima[:, conv - 1, m, cols],
                    scalar1=1.0,
                    scalar2=column,
                    op0=ALU.mult,
                    op1=ALU.add,
                )

        def store_pooled(conv, first, last):
            cols = slice(first * POOLED, (last + 1) * POOLED)
            nc.sync.dma_start(out=out_view[conv][:, :, cols], in_=pooled[:, conv - 1, :, cols])

        nc.scalar.dma_start(out=x_scales[:], in_=scale_view)
        nc.gpsimd.memset(warm[:], 0.0)
        nc.scalar.activation(out=warm[:, 1:2], in_=warm[:, 0:1], func=ACT.Copy, scale=1.0)
        make_identity(nc, ident[:])

        load_x_by_slot_pairs(0)
        for j in range(0, 2 * RUN):
            load_w(j)
        load_bias(THETA)
        load_x(1)
        for j in range(2 * RUN, TILES):
            load_w(j)
        for conv in (G, PHI):
            load_bias(conv)
        load_x(2)
        load_x(3)

        for t in (2, 3, 1):
            widen(0, 0, t, "vector")
        widen(0, 1, 1, "vector")
        widen(0, 0, 0, "scalar")
        for t in (0, 2, 3):
            widen(0, 1, t, "scalar")
        for j in range(2 * RUN):
            transpose_w(j)
        for j in range(2 * RUN):
            copy_w(j, "scalar")
        for g in range(PASSES):
            interleave(0, g, "vector")
        quantize_w_tile(0)
        quantize_x(0)
        quantize_w_tile(1)
        for q in range(1, RUN - 1):
            quantize_w(q)
        for t in range(PACK):
            widen(1, 0, t, "vector")
        quantize_w(RUN - 1)
        interleave(1, 0, "gpsimd")
        widen_pool_biases()
        for c in range(CHUNKS):
            for m in range(M_TILES):
                multiply(3 * m + THETA, c)
                finish_theta(m, c)
                if c == 0 and m == 0:
                    for t in range(PACK):
                        widen(1, 1, t, "scalar")
                elif c == 0 and m >= 2:
                    if m == 2:
                        quantize_x(1)
                    for t in range(PACK):
                        widen(2, m - 2, t, "scalar")
                    if m == 2:
                        interleave(2, 0, "gpsimd")
                elif 0 < c and c + 2 < CHUNKS:
                    for plane in (2 * m, 2 * m + 1):
                        widen(c + 2, plane // PACK, plane % PACK, "scalar")
                elif c == CHUNKS - 2:
                    for conv in (G, PHI):
                        add_pool_bias(conv, m, 0, 1, "scalar")
                    if m == M_TILES - 1:
                        for conv in (G, PHI):
                            store_pooled(conv, 0, 1)
                elif c == CHUNKS - 1 and m < 2:
                    for tile in (2 * m, 2 * m + 1):
                        for conv in (G, PHI):
                            add_pool_bias(conv, tile, 2, 2, "scalar")
                    if m == 1:
                        for conv in (G, PHI):
                            store_pooled(conv, 2, 2)
                if m == 1 and 0 < c and c + 1 < CHUNKS:
                    interleave(c + 1, 1, "vector")
                if c < CHUNKS - 1:
                    pair = ((G, m), (PHI, m))
                else:
                    conv = G if m < 2 else PHI
                    pair = ((conv, 2 * m % M_TILES), (conv, 2 * m % M_TILES + 1))
                for conv, tile in pair:
                    multiply(3 * tile + conv, c)
                    pool(conv, tile, c)
                    if c == 0 and m == 1:
                        half = RUN // 2
                        first = 2 * RUN + (0 if conv == G else half)
                        for j in range(first, first + half):
                            transpose_w(j)
                    if c == CHUNKS - 1:
                        add_pool_bias(conv, tile, c, c, "gpsimd")
                if c == CHUNKS - 1 and m in (1, 3):
                    store_pooled(G if m == 1 else PHI, c, c)
                if c == 0 and m == 1:
                    interleave(1, 1, "vector")
                    for j in range(2 * RUN, TILES):
                        copy_w(j, "scalar")
                        if j % 2 == 1:
                            quantize_w(j // 2)
                if m == 1 and 0 < c and c + 1 < CHUNKS:
                    quantize_x(c + 1)
                if m == 1 and 0 < c and c + 2 < CHUNKS:
                    interleave(c + 2, 0, "gpsimd")
